import numpy as np
import ml_dtypes


def mxq(x, axis, fmt="e4m3"):
    dtype, down = {"e4m3": (ml_dtypes.float8_e4m3fn, 7), "e5m2": (ml_dtypes.float8_e5m2, 14)}[fmt]
    v = np.moveaxis(np.asarray(x, np.float32).astype(ml_dtypes.bfloat16).astype(np.float64), axis, -1)
    blocks = v.reshape(v.shape[:-1] + (-1, 32))
    amax = np.abs(blocks).max(-1, keepdims=True)
    byte = np.maximum(np.where(amax > 0, np.frexp(amax)[1] - 1 + 127, 0) - down, 1)
    scale = np.exp2(byte - 127.0)
    codes = (blocks / scale).astype(np.float32).astype(dtype).astype(np.float64)
    return np.moveaxis((codes * scale).reshape(v.shape), -1, axis)


WIDE = False


def mx_kscale(k):
    if not WIDE:
        return np.ones(k)
    levels = np.array([10, -10, 5, -5, 0])
    if k % 512:
        return np.exp2(np.random.permutation(np.resize(levels, k // 32))).repeat(32)
    a = np.empty((k // 512, 16))
    for p in range(k // 512):
        a[p, :8] = np.random.permutation(np.resize(levels, 8))
        for g in range(8):
            far = levels[np.abs(levels - a[p, g]) >= 10]
            a[p, g + 8] = far[np.random.randint(len(far))]
    return np.exp2(a.ravel()).repeat(32)


BF16 = ml_dtypes.bfloat16


def bf(x):
    return np.asarray(x, np.float32).astype(BF16)


def f64(x):
    return np.asarray(x).astype(np.float64)


B, D, S, N = 1024, 2048, 4, 128
DS = D // S
EPS = 1e-12


def setup_inputs():
    s, t = mx_kscale(D), mx_kscale(D)
    return {"h": bf(np.random.standard_normal((B, D)) * s),
            "x2f": bf(np.random.standard_normal((B, D)) * t),
            "vu": bf(np.random.standard_normal((N, S, DS)) * 2.0 / np.sqrt(DS) / t.reshape(S, DS)),
            "w_f": bf(np.random.standard_normal((D, D)) / np.sqrt(D) * t[:, None] / s),
            "b_f": bf(np.random.standard_normal(D) * 0.2 * t),
            "bh": bf(1.0 + 0.1 * np.random.standard_normal(1)),
            "bx": bf(1.0 + 0.1 * np.random.standard_normal(1))}


def reference(h, x2f, vu, w_f, b_f, bh, bx):
    h2f = (mxq(f64(h), 1, "e4m3") @ mxq(f64(w_f), 1, "e4m3").T) + f64(b_f)
    vuq = mxq(f64(vu), 2, "e4m3").transpose(1, 2, 0)
    ah = (mxq(f64(x2f).reshape(B, S, DS), 2, "e4m3").transpose(1, 0, 2) @ vuq).transpose(1, 2, 0)
    ax = (mxq(h2f.reshape(B, S, DS), 2, "e4m3").transpose(1, 0, 2) @ vuq).transpose(1, 2, 0)
    ah = np.maximum(ah + f64(bh), 0.0)
    ax = np.maximum(ax + f64(bx), 0.0)
    a2 = (ah + ax) ** 2
    return a2 / np.maximum(a2.sum(axis=1, keepdims=True), EPS)

@@ -1,0 +1,292 @@
+from contextlib import ExitStack
+
+import concourse.mybir as mybir
+from concourse.masks import make_identity
+
+F32 = mybir.dt.float32
+BF16 = mybir.dt.bfloat16
+U32 = mybir.dt.uint32
+U8 = mybir.dt.uint8
+FP8X4 = mybir.dt.float8_e4m3fn_x4
+ACT = mybir.ActivationFunctionType
+ALU = mybir.AluOpType
+
+P = 128
+PACK = 4
+HALVES = 2
+K_PASS = P * PACK
+
+B, D, S, N = 1024, 2048, 4, 128
+DS = D // S
+PASSES = D // K_PASS
+ROW_TILES = B // P
+EPS = 1e-12
+
+FLOPS = 2 * B * D * D + 2 * (2 * B * D * N)
+
+EARLY = 2
+PACK_LEAD = 3
+SCORE_LAG = 3
+COMBINE_LAG = 4
+SQUARE_LAG = 5
+NORMALISE_LAG = 6
+
+
+def tile_tpru_pa_kernel(tc, h, x2f, vu, w_f, b_f, bh, bx, out):
+    nc = tc.nc
+    units = [(i, s) for s in range(S) for i in range(EARLY)]
+    units += [(i, s) for i in range(EARLY, ROW_TILES) for s in range(S)]
+    steps = range(-PACK_LEAD, len(units) + NORMALISE_LAG)
+
+    def is_unit(k):
+        return 0 <= k < len(units)
+
+    with ExitStack() as ctx:
+        keep = ctx.enter_context(tc.tile_pool(name="keep", bufs=1))
+        rows_pool = ctx.enter_context(tc.tile_pool(name="rows_pool", bufs=4))
+        flip_pool = ctx.enter_context(tc.tile_pool(name="flip_pool", bufs=6))
+        code_pool = ctx.enter_context(tc.tile_pool(name="code_pool", bufs=EARLY + 2))
+        feat_pool = ctx.enter_context(tc.tile_pool(name="feat_pool", bufs=4))
+        relu_pool = ctx.enter_context(tc.tile_pool(name="relu_pool", bufs=EARLY + 2))
+        work = ctx.enter_context(tc.tile_pool(name="work", bufs=2))
+        flip_psum = ctx.enter_context(tc.psum_pool(name="flip_psum", bufs=5))
+        feat_psum = ctx.enter_context(tc.psum_pool(name="feat_psum", bufs=3))
+        ctx.enter_context(tc.manual_schedule())
+
+        w_rows = {}
+        h_rows = {}
+        x_rows = {}
+        for k, (i, s) in enumerate(units):
+            if s == 0:
+                rows = rows_pool.tile([P, D], BF16, tag="h_rows", name="h_rows%d" % i)
+                nc.sync.dma_start(out=rows[:], in_=h[i * P : (i + 1) * P, :])
+                h_rows[i] = rows
+            if i == 0:
+                slice_rows = w_f[s * DS : (s + 1) * DS, :].rearrange("(r t) k -> t r k", t=PACK)
+                for t in range(PACK):
+                    rows = keep.tile([P, D], BF16, name="w_rows%d%d" % (s, t))
+                    nc.sync.dma_start(out=rows[:], in_=slice_rows[t])
+                    w_rows[(s, t)] = rows
+            if s == S - 1:
+                rows = rows_pool.tile([P, D], BF16, tag="x_rows", name="x_rows%d" % i)
+                nc.sync.dma_start(out=rows[:], in_=x2f[i * P : (i + 1) * P, :])
+                x_rows[i] = rows
+            if k == EARLY - 1:
+                vu_rows = keep.tile([P, D], BF16)
+                nc.sync.dma_start(out=vu_rows[:], in_=vu.rearrange("n s d -> n (s d)"))
+
+        ident = keep.tile([P, P], F32)
+        make_identity(nc, ident[:])
+        bias_bf = keep.tile([P, S, PACK], BF16)
+        nc.scalar.dma_start(out=bias_bf[:], in_=b_f.rearrange("(s p t) -> p s t", s=S, p=P))
+        bias = keep.tile([P, S, PACK], F32)
+        nc.vector.tensor_copy(out=bias[:], in_=bias_bf[:])
+        bh_bf = keep.tile([P, 1], BF16)
+        nc.scalar.dma_start(out=bh_bf[:], in_=bh.partition_broadcast(P))
+        bh_all = keep.tile([P, 1], F32)
+        nc.vector.tensor_copy(out=bh_all[:], in_=bh_bf[:])
+        bx_bf = keep.tile([P, 1], BF16)
+        nc.scalar.dma_start(out=bx_bf[:], in_=bx.partition_broadcast(P))
+        bx_all = keep.tile([P, 1], F32)
+        nc.vector.tensor_copy(out=bx_all[:], in_=bx_bf[:])
+
+        vu_codes = keep.tile([P, S, N], U32, align_bytes=64)
+        vu_scales = keep.tile([P, S, N], U8, align_bytes=64)
+        w_codes = keep.tile([P, S, PACK, PASSES, P], U32, align_bytes=64)
+        w_scales = keep.tile([P, S, PACK, PASSES, P], U8, align_bytes=64)
+
+        flipped_at = {k: [] for k in steps}
+        h_packed = {}
+        x_packed = {}
+        feat_of = {}
+        f_grouped_of = {}
+        both_of = {}
+        f_packed = {}
+        relu_x_of = {}
+        relu_h_of = {}
+        squared_of = {}
+
+        def flip(k, rows, codes, scales):
+            words = rows.bitcast(F32)
+            grouped = flip_pool.tile([P, PASSES, P, HALVES], F32, align_bytes=64)
+            for first in range(0, PASSES, 2):
+                flipped = flip_psum.tile([P, 2, HALVES, P], F32)
+                for g in range(2):
+                    for u in range(HALVES):
+                        column = (first + g) * HALVES * P
+                        nc.tensor.transpose(
+                            flipped[:, g, u, :],
+                            words[:, column + u : column + HALVES * P : HALVES],
+                            ident[:],
+                        )
+                nc.scalar.copy(
+                    out=grouped[:, first : first + 2, :, :],
+                    in_=flipped[:].rearrange("q g u r -> q g r u"),
+                )
+            flipped_at[k].append((grouped, codes, scales))
+
+        def quantise_flipped(k):
+            for grouped, codes, scales in flipped_at.get(k, []):
+                nc.vector.quantize_mx(
+                    out=codes.rearrange("q g r -> q (g r)").bitcast(FP8X4),
+                    scales=scales.rearrange("q g r -> q (g r)"),
+                    in_=grouped[:].rearrange("q g r u -> q (g r u)").bitcast(BF16),
+                )
+
+        def flip_ahead(k):
+            ahead = k + PACK_LEAD
+            if is_unit(ahead) and units[ahead][1] == 0:
+                i = units[ahead][0]
+                h_codes = code_pool.tile([P, PASSES, P], U32, align_bytes=64)
+                h_scales = code_pool.tile([P, PASSES, P], U8, align_bytes=64)
+                flip(k, h_rows[i][:], h_codes[:], h_scales[:])
+                h_packed[i] = (h_codes, h_scales)
+            for u in range(HALVES):
+                ahead = k + PACK_LEAD - u
+                if is_unit(ahead) and units[ahead][0] == 0:
+                    s = units[ahead][1]
+                    for t in range(2 * u, 2 * u + 2):
+                        flip(k, w_rows[(s, t)][:], w_codes[:, s, t], w_scales[:, s, t])
+            ahead = k + PACK_LEAD - 1
+            if is_unit(ahead) and units[ahead][1] == S - 1:
+                i = units[ahead][0]
+                x_codes = code_pool.tile([P, S, P], U32, align_bytes=64)
+                x_scales = code_pool.tile([P, S, P], U8, align_bytes=64)
+                flip(k, x_rows[i][:], x_codes[:], x_scales[:])
+                x_packed[i] = (x_codes, x_scales)
+            if k == 0:
+                flip(k, vu_rows[:], vu_codes[:], vu_scales[:])
+
+        def features(k):
+            i, s = units[k]
+            h_codes, h_scales = h_packed[i]
+            feat = feat_psum.tile([P, PACK, P], F32)
+            for t in range(PACK):
+                for g in range(PASSES):
+                    nc.tensor.matmul_mx(
+                        out=feat[:, t, :],
+                        lhsT=w_codes[:, s, t, g, :].bitcast(FP8X4),
+                        lhsT_scale=w_scales[:, s, t, g, :],
+                        rhs=h_codes[:, g, :].bitcast(FP8X4),
+                        rhs_scale=h_scales[:, g, :],
+                        start=(g == 0),
+                        stop=(g == PASSES - 1),
+                    )
+            feat_of[k] = feat
+
+        def add_bias(k):
+            s = units[k][1]
+            feat = feat_of[k]
+            f_grouped = feat_pool.tile([P, P, PACK], BF16, align_bytes=64)
+            nc.vector.tensor_tensor(
+                out=f_grouped[:],
+                in0=feat[:].rearrange("p t b -> p b t"),
+                in1=bias[:, s, :].unsqueeze(1).to_broadcast([P, P, PACK]),
+                op=ALU.add,
+            )
+            f_grouped_of[k] = f_grouped
+
+        def quantise_features(k):
+            f_codes = feat_pool.tile([P, P], U32, align_bytes=64)
+            f_scales = feat_pool.tile([P, P], U8, align_bytes=64)
+            nc.vector.quantize_mx(
+                out=f_codes[:].bitcast(FP8X4),
+                scales=f_scales[:],
+                in_=f_grouped_of[k][:].rearrange("p b t -> p (b t)"),
+            )
+            f_packed[k] = (f_codes, f_scales)
+
+        def scores(k):
+            i, s = units[k]
+            if s == S - 1:
+                x_codes, x_scales = x_packed[i]
+                ah = flip_psum.tile([P, S, N], F32, tag="flipped")
+                for j in range(S):
+                    nc.tensor.matmul_mx(
+                        out=ah[:, j, :],
+                        lhsT=x_codes[:, j, :].bitcast(FP8X4),
+                        lhsT_scale=x_scales[:, j, :],
+                        rhs=vu_codes[:, j, :].bitcast(FP8X4),
+                        rhs_scale=vu_scales[:, j, :],
+                        start=True,
+                        stop=True,
+                    )
+                relu_h = work.tile([P, S, N], F32)
+                nc.scalar.activation(
+                    out=relu_h[:], in_=ah[:], func=ACT.Relu, bias=bh_all[:], scale=1.0
+                )
+                relu_h_of[i] = relu_h
+            if s == 0:
+                relu_x = relu_pool.tile([P, S, N], F32)
+                relu_x_of[i] = relu_x
+            f_codes, f_scales = f_packed[k]
+            ax = flip_psum.tile([P, N], F32, tag="flipped")
+            nc.tensor.matmul_mx(
+                out=ax[:],
+                lhsT=f_codes[:].bitcast(FP8X4),
+                lhsT_scale=f_scales[:],
+                rhs=vu_codes[:, s, :].bitcast(FP8X4),
+                rhs_scale=vu_scales[:, s, :],
+                start=True,
+                stop=True,
+            )
+            nc.scalar.activation(
+                out=relu_x_of[i][:, s, :], in_=ax[:], func=ACT.Relu, bias=bx_all[:], scale=1.0
+            )
+
+        def combine(i):
+            both = work.tile([P, S, N], F32)
+            nc.vector.tensor_add(out=both[:], in0=relu_h_of[i][:], in1=relu_x_of[i][:])
+            both_of[i] = both
+
+        def square(i):
+            both = both_of[i]
+            squared = work.tile([P, S, N], F32)
+            total = work.tile([P, S], F32)
+            for s in range(S):
+                nc.scalar.activation(
+                    out=squared[:, s, :],
+                    in_=both[:, s, :],
+                    func=ACT.Square,
+                    accum_out=total[:, s : s + 1],
+                )
+            squared_of[i] = (squared, total)
+
+        def normalise(i):
+            squared, total = squared_of[i]
+            floored = work.tile([P, S], F32)
+            nc.vector.tensor_scalar_max(out=floored[:], in0=total[:], scalar1=EPS)
+            inverse = work.tile([P, S], F32)
+            nc.vector.reciprocal(out=inverse[:], in_=floored[:])
+            share = work.tile([P, N, S], F32)
+            nc.vector.tensor_tensor(
+                out=share[:],
+                in0=squared[:].rearrange("p s n -> p n s"),
+                in1=inverse[:].unsqueeze(1).to_broadcast([P, N, S]),
+                op=ALU.mult,
+            )
+            nc.sync.dma_start(
+                out=out[i * P : (i + 1) * P].rearrange("b n s -> b (n s)"),
+                in_=share[:].rearrange("p n s -> p (n s)"),
+            )
+
+        def ends_row_tile(k):
+            return is_unit(k) and units[k][1] == S - 1
+
+        for k in steps:
+            if is_unit(k):
+                features(k)
+            quantise_flipped(k - 1)
+            if ends_row_tile(k - COMBINE_LAG):
+                combine(units[k - COMBINE_LAG][0])
+            if ends_row_tile(k - NORMALISE_LAG):
+                normalise(units[k - NORMALISE_LAG][0])
+            if is_unit(k - 1):
+                quantise_features(k - 1)
+            if is_unit(k):
+                add_bias(k)
+            flip_ahead(k)
+            if is_unit(k - SCORE_LAG):
+                scores(k - SCORE_LAG)
+            if ends_row_tile(k - SQUARE_LAG):
+                square(units[k - SQUARE_LAG][0])

@@ -25,55 +25,64 @@ EPS = 1e-12
 FLOPS = 2 * B * D * D + 2 * (2 * B * D * N)
 
 EARLY = 2
-PACK_LEAD = 3
-SCORE_LAG = 3
-COMBINE_LAG = 4
-SQUARE_LAG = 5
-NORMALISE_LAG = 6
+EARLY_STEPS = S * EARLY
+STEPS = EARLY_STEPS + (ROW_TILES - EARLY) * S
+HALF = PACK // EARLY
+LOAD_LEAD = 10
 
 
 def tile_tpru_pa_kernel(tc, h, x2f, vu, w_f, b_f, bh, bx, out):
     nc = tc.nc
-    units = [(i, s) for s in range(S) for i in range(EARLY)]
-    units += [(i, s) for i in range(EARLY, ROW_TILES) for s in range(S)]
-    steps = range(-PACK_LEAD, len(units) + NORMALISE_LAG)
 
-    def is_unit(k):
-        return 0 <= k < len(units)
+    def first_step(i):
+        return 0 if i < EARLY else EARLY_STEPS + (i - EARLY) * S
+
+    flips = {k: [] for k in range(-2, STEPS)}
+    flips[-2] = [("h", 0, 0), ("w", 0, 0), ("w", 0, 1)]
+    flips[-1] = [("h", 1, 0), ("w", 0, 2), ("w", 0, 3)]
+    for s in range(1, S):
+        for t in range(PACK):
+            flips[EARLY * (s - 1) + t // HALF].append(("w", s, t))
+    flips[EARLY_STEPS - 2] = [("h", EARLY, 0), ("vu", 0, 0)]
+    flips[EARLY_STEPS - 1] = [("x", EARLY, 0)]
+    for i in range(EARLY + 1, ROW_TILES):
+        flips[first_step(i) - 3] = [("h", i, 0), ("x", i, 0)]
+    for i in range(EARLY):
+        flips[first_step(EARLY + i) + 3] = [("x", i, 0)]
 
     with ExitStack() as ctx:
         keep = ctx.enter_context(tc.tile_pool(name="keep", bufs=1))
         rows_pool = ctx.enter_context(tc.tile_pool(name="rows_pool", bufs=4))
+        w_pool = ctx.enter_context(tc.tile_pool(name="w_pool", bufs=3 * PACK))
+        order_pool = ctx.enter_context(tc.tile_pool(name="order_pool", bufs=3))
         flip_pool = ctx.enter_context(tc.tile_pool(name="flip_pool", bufs=6))
-        code_pool = ctx.enter_context(tc.tile_pool(name="code_pool", bufs=EARLY + 2))
+        code_pool = ctx.enter_context(tc.tile_pool(name="code_pool", bufs=4))
         feat_pool = ctx.enter_context(tc.tile_pool(name="feat_pool", bufs=4))
-        relu_pool = ctx.enter_context(tc.tile_pool(name="relu_pool", bufs=EARLY + 2))
-        work = ctx.enter_context(tc.tile_pool(name="work", bufs=2))
-        flip_psum = ctx.enter_context(tc.psum_pool(name="flip_psum", bufs=5))
-        feat_psum = ctx.enter_context(tc.psum_pool(name="feat_psum", bufs=3))
+        fcode_pool = ctx.enter_context(tc.tile_pool(name="fcode_pool", bufs=(EARLY + 3) * S))
+        work = ctx.enter_context(tc.tile_pool(name="work", bufs=3))
+        flip_psum = ctx.enter_context(tc.psum_pool(name="flip_psum", bufs=4))
+        feat_psum = ctx.enter_context(tc.psum_pool(name="feat_psum", bufs=4))
         ctx.enter_context(tc.manual_schedule())
 
-        w_rows = {}
-        h_rows = {}
-        x_rows = {}
-        for k, (i, s) in enumerate(units):
-            if s == 0:
-                rows = rows_pool.tile([P, D], BF16, tag="h_rows", name="h_rows%d" % i)
-                nc.sync.dma_start(out=rows[:], in_=h[i * P : (i + 1) * P, :])
-                h_rows[i] = rows
-            if i == 0:
-                slice_rows = w_f[s * DS : (s + 1) * DS, :].rearrange("(r t) k -> t r k", t=PACK)
-                for t in range(PACK):
-                    rows = keep.tile([P, D], BF16, name="w_rows%d%d" % (s, t))
-                    nc.sync.dma_start(out=rows[:], in_=slice_rows[t])
-                    w_rows[(s, t)] = rows
-            if s == S - 1:
-                rows = rows_pool.tile([P, D], BF16, tag="x_rows", name="x_rows%d" % i)
-                nc.sync.dma_start(out=rows[:], in_=x2f[i * P : (i + 1) * P, :])
-                x_rows[i] = rows
-            if k == EARLY - 1:
-                vu_rows = keep.tile([P, D], BF16)
-                nc.sync.dma_start(out=vu_rows[:], in_=vu.rearrange("n s d -> n (s d)"))
+        rows_of = {}
+
+        def load(k):
+            for tile in flips.get(k, []):
+                kind, i, t = tile
+                if kind == "w":
+                    source = w_f[i * DS : (i + 1) * DS, :].rearrange("(r t) k -> t r k", t=PACK)[t]
+                    rows = w_pool.tile([P, D], BF16, tag="w_rows", name="w_rows")
+                elif kind == "vu":
+                    source = vu.rearrange("n s d -> n (s d)")
+                    rows = keep.tile([P, D], BF16, name="vu_rows")
+                else:
+                    source = (h if kind == "h" else x2f)[i * P : (i + 1) * P, :]
+                    rows = rows_pool.tile([P, D], BF16, tag=kind + "_rows", name="rows")
+                nc.sync.dma_start(out=rows[:], in_=source)
+                rows_of[tile] = rows
+
+        for k in range(-2, LOAD_LEAD - 2):
+            load(k)
 
         ident = keep.tile([P, P], F32)
         make_identity(nc, ident[:])
@@ -89,175 +98,225 @@ def tile_tpru_pa_kernel(tc, h, x2f, vu, w_f, b_f, bh, bx, out):
         nc.scalar.dma_start(out=bx_bf[:], in_=bx.partition_broadcast(P))
         bx_all = keep.tile([P, 1], F32)
         nc.vector.tensor_copy(out=bx_all[:], in_=bx_bf[:])
+        minus_bx = keep.tile([P, 1], F32)
+        nc.vector.tensor_scalar_mul(out=minus_bx[:], in0=bx_bf[:], scalar1=-1.0)
 
         vu_codes = keep.tile([P, S, N], U32, align_bytes=64)
         vu_scales = keep.tile([P, S, N], U8, align_bytes=64)
         w_codes = keep.tile([P, S, PACK, PASSES, P], U32, align_bytes=64)
         w_scales = keep.tile([P, S, PACK, PASSES, P], U8, align_bytes=64)
 
-        flipped_at = {k: [] for k in steps}
-        h_packed = {}
-        x_packed = {}
+        ordered_of = {}
+        flipped_at = {k: [] for k in range(-3, STEPS + 1)}
+        packed = {}
         feat_of = {}
         f_grouped_of = {}
-        both_of = {}
         f_packed = {}
-        relu_x_of = {}
         relu_h_of = {}
+        ax_of = {}
+        both_of = {}
         squared_of = {}
+        floored_of = {}
+        inverse_of = {}
 
-        def flip(k, rows, codes, scales):
-            words = rows.bitcast(F32)
-            grouped = flip_pool.tile([P, PASSES, P, HALVES], F32, align_bytes=64)
-            for first in range(0, PASSES, 2):
-                flipped = flip_psum.tile([P, 2, HALVES, P], F32)
-                for g in range(2):
-                    for u in range(HALVES):
-                        column = (first + g) * HALVES * P
-                        nc.tensor.transpose(
-                            flipped[:, g, u, :],
-                            words[:, column + u : column + HALVES * P : HALVES],
-                            ident[:],
-                        )
-                nc.scalar.copy(
-                    out=grouped[:, first : first + 2, :, :],
-                    in_=flipped[:].rearrange("q g u r -> q g r u"),
-                )
-            flipped_at[k].append((grouped, codes, scales))
+        def packed_for(tile):
+            kind, i, t = tile
+            if kind == "w":
+                return w_codes[:, i, t], w_scales[:, i, t]
+            if kind == "vu":
+                return vu_codes[:], vu_scales[:]
+            codes = code_pool.tile(
+                [P, PASSES, P], U32, tag=kind + "_codes", name="codes", align_bytes=64
+            )
+            scales = code_pool.tile(
+                [P, PASSES, P], U8, tag=kind + "_scales", name="scales", align_bytes=64
+            )
+            packed[(kind, i)] = (codes, scales)
+            return codes[:], scales[:]
+
+        def orderer(tile):
+            kind, i, t = tile
+            if kind == "w":
+                if EARLY * i + t // HALF <= EARLY:
+                    return None
+                return "scalar" if i > 1 and t == PACK - 1 else "vector"
+            if kind == "h":
+                return None if i < EARLY else "scalar"
+            return "vector" if kind == "vu" or (i >= EARLY and i % 2 == 0) else "scalar"
+
+        def words_by_half(tile):
+            return rows_of[tile][:].bitcast(F32).rearrange("r (g q u) -> r g u q", g=PASSES, u=HALVES)
+
+        reorders = {k: [] for k in range(-3, STEPS)}
+        for k in range(-2, STEPS):
+            for n, tile in enumerate(flips[k]):
+                if orderer(tile) == "vector":
+                    reorders[k - 1].append(tile)
+                elif orderer(tile) == "scalar":
+                    reorders[k - 2].append(tile)
+
+        def reorder(k, who, copy):
+            for tile in reorders[k]:
+                if orderer(tile) == who:
+                    ordered = order_pool.tile(
+                        [P, PASSES, HALVES, P], F32, tag="ordered_" + who, align_bytes=64
+                    )
+                    copy(out=ordered[:], in_=words_by_half(tile))
+                    ordered_of[tile] = ordered
+
+        def flip(k):
+            for tile in flips.get(k, []):
+                halves = ordered_of[tile][:] if tile in ordered_of else words_by_half(tile)
+                grouped = flip_pool.tile([P, PASSES, P, HALVES], F32, align_bytes=64)
+                for first in range(0, PASSES, 2):
+                    flipped = flip_psum.tile([P, 2, HALVES, P], F32)
+                    for g in range(2):
+                        for u in range(HALVES):
+                            nc.tensor.transpose(
+                                flipped[:, g, u, :], halves[:, first + g, u, :], ident[:]
+                            )
+                    nc.scalar.copy(
+                        out=grouped[:, first : first + 2, :, :],
+                        in_=flipped[:].rearrange("q g u r -> q g r u"),
+                    )
+                flipped_at[k].append((tile, grouped))
 
         def quantise_flipped(k):
-            for grouped, codes, scales in flipped_at.get(k, []):
+            for tile, grouped in flipped_at.get(k, []):
+                codes, scales = packed_for(tile)
                 nc.vector.quantize_mx(
                     out=codes.rearrange("q g r -> q (g r)").bitcast(FP8X4),
                     scales=scales.rearrange("q g r -> q (g r)"),
                     in_=grouped[:].rearrange("q g r u -> q (g r u)").bitcast(BF16),
                 )
 
-        def flip_ahead(k):
-            ahead = k + PACK_LEAD
-            if is_unit(ahead) and units[ahead][1] == 0:
-                i = units[ahead][0]
-                h_codes = code_pool.tile([P, PASSES, P], U32, align_bytes=64)
-                h_scales = code_pool.tile([P, PASSES, P], U8, align_bytes=64)
-                flip(k, h_rows[i][:], h_codes[:], h_scales[:])
-                h_packed[i] = (h_codes, h_scales)
-            for u in range(HALVES):
-                ahead = k + PACK_LEAD - u
-                if is_unit(ahead) and units[ahead][0] == 0:
-                    s = units[ahead][1]
-                    for t in range(2 * u, 2 * u + 2):
-                        flip(k, w_rows[(s, t)][:], w_codes[:, s, t], w_scales[:, s, t])
-            ahead = k + PACK_LEAD - 1
-            if is_unit(ahead) and units[ahead][1] == S - 1:
-                i = units[ahead][0]
-                x_codes = code_pool.tile([P, S, P], U32, align_bytes=64)
-                x_scales = code_pool.tile([P, S, P], U8, align_bytes=64)
-                flip(k, x_rows[i][:], x_codes[:], x_scales[:])
-                x_packed[i] = (x_codes, x_scales)
-            if k == 0:
-                flip(k, vu_rows[:], vu_codes[:], vu_scales[:])
+        def step_work(k):
+            if k < EARLY_STEPS:
+                half = k % EARLY
+                return range(EARLY), k // EARLY, range(half * HALF, (half + 1) * HALF)
+            i, s = divmod(k - EARLY_STEPS, S)
+            return (i + EARLY,), s, range(PACK)
+
+        def finished(k):
+            if not 0 <= k < STEPS:
+                return []
+            row_tiles, s, tiles = step_work(k)
+            return [(i, s) for i in row_tiles] if PACK - 1 in tiles else []
 
         def features(k):
-            i, s = units[k]
-            h_codes, h_scales = h_packed[i]
-            feat = feat_psum.tile([P, PACK, P], F32)
-            for t in range(PACK):
+            row_tiles, s, tiles = step_work(k)
+            for i in row_tiles:
+                if 0 in tiles:
+                    feat = feat_psum.tile([P, PACK, P], F32)
+                    feat_of[(i, s)] = feat
+            for t in tiles:
                 for g in range(PASSES):
-                    nc.tensor.matmul_mx(
-                        out=feat[:, t, :],
-                        lhsT=w_codes[:, s, t, g, :].bitcast(FP8X4),
-                        lhsT_scale=w_scales[:, s, t, g, :],
-                        rhs=h_codes[:, g, :].bitcast(FP8X4),
-                        rhs_scale=h_scales[:, g, :],
-                        start=(g == 0),
-                        stop=(g == PASSES - 1),
-                    )
-            feat_of[k] = feat
+                    for i in row_tiles:
+                        h_codes, h_scales = packed[("h", i)]
+                        nc.tensor.matmul_mx(
+                            out=feat_of[(i, s)][:, t, :],
+                            lhsT=w_codes[:, s, t, g, :].bitcast(FP8X4),
+                            lhsT_scale=w_scales[:, s, t, g, :],
+                            rhs=h_codes[:, g, :].bitcast(FP8X4),
+                            rhs_scale=h_scales[:, g, :],
+                            start=(g == 0),
+                            stop=(g == PASSES - 1),
+                        )
 
         def add_bias(k):
-            s = units[k][1]
-            feat = feat_of[k]
-            f_grouped = feat_pool.tile([P, P, PACK], BF16, align_bytes=64)
-            nc.vector.tensor_tensor(
-                out=f_grouped[:],
-                in0=feat[:].rearrange("p t b -> p b t"),
-                in1=bias[:, s, :].unsqueeze(1).to_broadcast([P, P, PACK]),
-                op=ALU.add,
-            )
-            f_grouped_of[k] = f_grouped
+            for i, s in finished(k):
+                f_grouped = feat_pool.tile([P, P, PACK], BF16, align_bytes=64)
+                nc.vector.tensor_tensor(
+                    out=f_grouped[:],
+                    in0=feat_of[(i, s)][:].rearrange("p t b -> p b t"),
+                    in1=bias[:, s, :].unsqueeze(1).to_broadcast([P, P, PACK]),
+                    op=ALU.add,
+                )
+                f_grouped_of[(i, s)] = f_grouped
 
         def quantise_features(k):
-            f_codes = feat_pool.tile([P, P], U32, align_bytes=64)
-            f_scales = feat_pool.tile([P, P], U8, align_bytes=64)
-            nc.vector.quantize_mx(
-                out=f_codes[:].bitcast(FP8X4),
-                scales=f_scales[:],
-                in_=f_grouped_of[k][:].rearrange("p b t -> p (b t)"),
-            )
-            f_packed[k] = (f_codes, f_scales)
-
-        def scores(k):
-            i, s = units[k]
-            if s == S - 1:
-                x_codes, x_scales = x_packed[i]
-                ah = flip_psum.tile([P, S, N], F32, tag="flipped")
-                for j in range(S):
-                    nc.tensor.matmul_mx(
-                        out=ah[:, j, :],
-                        lhsT=x_codes[:, j, :].bitcast(FP8X4),
-                        lhsT_scale=x_scales[:, j, :],
-                        rhs=vu_codes[:, j, :].bitcast(FP8X4),
-                        rhs_scale=vu_scales[:, j, :],
-                        start=True,
-                        stop=True,
-                    )
-                relu_h = work.tile([P, S, N], F32)
-                nc.scalar.activation(
-                    out=relu_h[:], in_=ah[:], func=ACT.Relu, bias=bh_all[:], scale=1.0
+            for i, s in finished(k):
+                f_codes = fcode_pool.tile([P, P], U32, align_bytes=64)
+                f_scales = fcode_pool.tile([P, P], U8, align_bytes=64)
+                nc.vector.quantize_mx(
+                    out=f_codes[:].bitcast(FP8X4),
+                    scales=f_scales[:],
+                    in_=f_grouped_of[(i, s)][:].rearrange("p b t -> p (b t)"),
                 )
-                relu_h_of[i] = relu_h
-            if s == 0:
-                relu_x = relu_pool.tile([P, S, N], F32)
-                relu_x_of[i] = relu_x
-            f_codes, f_scales = f_packed[k]
-            ax = flip_psum.tile([P, N], F32, tag="flipped")
+                f_packed[(i, s)] = (f_codes, f_scales)
+
+        def score(out_scores, s, codes, scales):
             nc.tensor.matmul_mx(
-                out=ax[:],
-                lhsT=f_codes[:].bitcast(FP8X4),
-                lhsT_scale=f_scales[:],
+                out=out_scores,
+                lhsT=codes.bitcast(FP8X4),
+                lhsT_scale=scales,
                 rhs=vu_codes[:, s, :].bitcast(FP8X4),
                 rhs_scale=vu_scales[:, s, :],
                 start=True,
                 stop=True,
             )
+
+        def scores_of_x(i):
+            x_codes, x_scales = packed[("x", i)]
+            ah = flip_psum.tile([P, S, N], F32, tag="flipped")
+            for s in range(S):
+                score(ah[:, s, :], s, x_codes[:, s, :], x_scales[:, s, :])
+            relu_h = work.tile([P, S, N], F32)
             nc.scalar.activation(
-                out=relu_x_of[i][:, s, :], in_=ax[:], func=ACT.Relu, bias=bx_all[:], scale=1.0
+                out=relu_h[:], in_=ah[:], func=ACT.Relu, bias=bh_all[:], scale=1.0
+            )
+            relu_h_of[i] = relu_h
+
+        def scores_of_features(i, slices):
+            if 0 in slices:
+                ax = flip_psum.tile([P, S, N], F32, tag="flipped")
+                ax_of[i] = ax
+            for s in slices:
+                f_codes, f_scales = f_packed[(i, s)]
+                score(ax_of[i][:, s, :], s, f_codes[:], f_scales[:])
+
+        def combine(i, first=0, last=S):
+            if first == 0:
+                both = work.tile([P, S, N], F32)
+                both_of[i] = both
+            nc.vector.scalar_tensor_tensor(
+                out=both_of[i][:, first:last, :],
+                in0=ax_of[i][:, first:last, :],
+                scalar=minus_bx[:],
+                in1=relu_h_of[i][:, first:last, :],
+                op0=ALU.max,
+                op1=ALU.add,
             )
 
-        def combine(i):
-            both = work.tile([P, S, N], F32)
-            nc.vector.tensor_add(out=both[:], in0=relu_h_of[i][:], in1=relu_x_of[i][:])
-            both_of[i] = both
-
-        def square(i):
-            both = both_of[i]
-            squared = work.tile([P, S, N], F32)
-            total = work.tile([P, S], F32)
-            for s in range(S):
+        def square(i, first=0, last=S):
+            if first == 0:
+                squared = work.tile([P, S, N], F32)
+                total = work.tile([P, S], F32)
+                squared_of[i] = (squared, total)
+            squared, total = squared_of[i]
+            for s in range(first, last):
                 nc.scalar.activation(
                     out=squared[:, s, :],
-                    in_=both[:, s, :],
+                    in_=both_of[i][:, s, :],
                     func=ACT.Square,
+                    bias=bx_all[:],
                     accum_out=total[:, s : s + 1],
                 )
-            squared_of[i] = (squared, total)
 
-        def normalise(i):
-            squared, total = squared_of[i]
+        def floor_total(i):
+            total = squared_of[i][1]
             floored = work.tile([P, S], F32)
             nc.vector.tensor_scalar_max(out=floored[:], in0=total[:], scalar1=EPS)
+            floored_of[i] = floored
+
+        def invert(i):
             inverse = work.tile([P, S], F32)
-            nc.vector.reciprocal(out=inverse[:], in_=floored[:])
+            nc.vector.reciprocal(out=inverse[:], in_=floored_of[i][:])
+            inverse_of[i] = inverse
+
+        def normalise(i):
+            squared = squared_of[i][0]
+            inverse = inverse_of[i]
             share = work.tile([P, N, S], F32)
             nc.vector.tensor_tensor(
                 out=share[:],
@@ -270,23 +329,49 @@ def tile_tpru_pa_kernel(tc, h, x2f, vu, w_f, b_f, bh, bx, out):
                 in_=share[:].rearrange("p n s -> p (n s)"),
             )
 
-        def ends_row_tile(k):
-            return is_unit(k) and units[k][1] == S - 1
-
-        for k in steps:
-            if is_unit(k):
-                features(k)
+        score_step = {i: first_step(i) + S + 2 for i in range(EARLY, ROW_TILES - 1)}
+        for i in range(EARLY):
+            score_step[i] = first_step(EARLY + i) + S + 3
+        scored_at = {k: i for i, k in score_step.items()}
+        LAST = ROW_TILES - 1
+        for k in range(-2, STEPS):
+            load(k + LOAD_LEAD)
+            if k - 3 in scored_at:
+                floor_total(scored_at[k - 3])
+            if k - 1 in scored_at:
+                combine(scored_at[k - 1])
+            quantise_features(k - 1)
+            if k - 3 in scored_at:
+                invert(scored_at[k - 3])
             quantise_flipped(k - 1)
-            if ends_row_tile(k - COMBINE_LAG):
-                combine(units[k - COMBINE_LAG][0])
-            if ends_row_tile(k - NORMALISE_LAG):
-                normalise(units[k - NORMALISE_LAG][0])
-            if is_unit(k - 1):
-                quantise_features(k - 1)
-            if is_unit(k):
+            if k >= 0:
+                features(k)
+            if k in scored_at:
+                scores_of_x(scored_at[k])
+                scores_of_features(scored_at[k], range(S))
+            if k == STEPS - 1:
+                scores_of_x(LAST)
+                scores_of_features(LAST, range(S - 1))
+            if k - 2 in scored_at:
+                square(scored_at[k - 2])
+            flip(k)
+            if k - 3 in scored_at:
+                normalise(scored_at[k - 3])
+            reorder(k, "vector", nc.vector.tensor_copy)
+            reorder(k, "scalar", nc.scalar.copy)
+            if k >= 0:
                 add_bias(k)
-            flip_ahead(k)
-            if is_unit(k - SCORE_LAG):
-                scores(k - SCORE_LAG)
-            if ends_row_tile(k - SQUARE_LAG):
-                square(units[k - SQUARE_LAG][0])
+        square(LAST - 1)
+        combine(LAST, 0, S - 2)
+        quantise_features(STEPS - 1)
+        scores_of_features(LAST, (S - 1,))
+        combine(LAST, S - 2, S - 1)
+        square(LAST, 0, S - 1)
+        floor_total(LAST - 1)
+        invert(LAST - 1)
+        combine(LAST, S - 1, S)
+        square(LAST, S - 1, S)
+        normalise(LAST - 1)
+        floor_total(LAST)
+        invert(LAST)
+        normalise(LAST)

@@ -29,6 +29,7 @@ EARLY_STEPS = S * EARLY
 STEPS = EARLY_STEPS + (ROW_TILES - EARLY) * S
 HALF = PACK // EARLY
 LOAD_LEAD = 10
+RUN = 8
 
 
 def tile_tpru_pa_kernel(tc, h, x2f, vu, w_f, b_f, bh, bx, out):
@@ -81,7 +82,7 @@ def tile_tpru_pa_kernel(tc, h, x2f, vu, w_f, b_f, bh, bx, out):
                 nc.sync.dma_start(out=rows[:], in_=source)
                 rows_of[tile] = rows
 
-        for k in range(-2, LOAD_LEAD - 2):
+        for k in range(-2, LOAD_LEAD - 3):
             load(k)
 
         ident = keep.tile([P, P], F32)
@@ -137,21 +138,22 @@ def tile_tpru_pa_kernel(tc, h, x2f, vu, w_f, b_f, bh, bx, out):
         def orderer(tile):
             kind, i, t = tile
             if kind == "w":
-                if EARLY * i + t // HALF <= EARLY:
-                    return None
                 return "scalar" if i > 1 and t == PACK - 1 else "vector"
             if kind == "h":
-                return None if i < EARLY else "scalar"
-            return "vector" if kind == "vu" or (i >= EARLY and i % 2 == 0) else "scalar"
+                return "vector" if i < EARLY else "scalar"
+            return None if kind == "vu" or i % 2 == 0 else "scalar"
 
         def words_by_half(tile):
-            return rows_of[tile][:].bitcast(F32).rearrange("r (g q u) -> r g u q", g=PASSES, u=HALVES)
+            words = rows_of[tile][:].bitcast(F32)
+            if tile[0] in ("h", "w"):
+                return words.rearrange("r (b u i) -> r u b i", u=HALVES, i=RUN)
+            return words.rearrange("r (b u) -> r u b", u=HALVES)
 
-        reorders = {k: [] for k in range(-3, STEPS)}
+        reorders = {k: [] for k in range(-4, STEPS)}
         for k in range(-2, STEPS):
             for n, tile in enumerate(flips[k]):
                 if orderer(tile) == "vector":
-                    reorders[k - 1].append(tile)
+                    reorders[k - 1 if k not in (0, 1) else 0].append(tile)
                 elif orderer(tile) == "scalar":
                     reorders[k - 2].append(tile)
 
@@ -159,9 +161,12 @@ def tile_tpru_pa_kernel(tc, h, x2f, vu, w_f, b_f, bh, bx, out):
             for tile in reorders[k]:
                 if orderer(tile) == who:
                     ordered = order_pool.tile(
-                        [P, PASSES, HALVES, P], F32, tag="ordered_" + who, align_bytes=64
+                        [P, HALVES, PASSES * P], F32, tag="ordered_" + who, align_bytes=64
                     )
-                    copy(out=ordered[:], in_=words_by_half(tile))
+                    laid = ordered[:]
+                    if tile[0] in ("h", "w"):
+                        laid = laid.rearrange("r u (b i) -> r u b i", i=RUN)
+                    copy(out=laid, in_=words_by_half(tile))
                     ordered_of[tile] = ordered
 
         def flip(k):
@@ -173,7 +178,9 @@ def tile_tpru_pa_kernel(tc, h, x2f, vu, w_f, b_f, bh, bx, out):
                     for g in range(2):
                         for u in range(HALVES):
                             nc.tensor.transpose(
-                                flipped[:, g, u, :], halves[:, first + g, u, :], ident[:]
+                                flipped[:, g, u, :],
+                                halves[:, u, (first + g) * P : (first + g + 1) * P],
+                                ident[:],
                             )
                     nc.scalar.copy(
                         out=grouped[:, first : first + 2, :, :],
@@ -334,7 +341,7 @@ def tile_tpru_pa_kernel(tc, h, x2f, vu, w_f, b_f, bh, bx, out):
             score_step[i] = first_step(EARLY + i) + S + 3
         scored_at = {k: i for i, k in score_step.items()}
         LAST = ROW_TILES - 1
-        for k in range(-2, STEPS):
+        for k in range(-3, STEPS):
             load(k + LOAD_LEAD)
             if k - 3 in scored_at:
                 floor_total(scored_at[k - 3])
@@ -344,6 +351,8 @@ def tile_tpru_pa_kernel(tc, h, x2f, vu, w_f, b_f, bh, bx, out):
             if k - 3 in scored_at:
                 invert(scored_at[k - 3])
             quantise_flipped(k - 1)
+            if k == 0:
+                reorder(k, "vector", nc.vector.tensor_copy)
             if k >= 0:
                 features(k)
             if k in scored_at:
@@ -357,7 +366,8 @@ def tile_tpru_pa_kernel(tc, h, x2f, vu, w_f, b_f, bh, bx, out):
             flip(k)
             if k - 3 in scored_at:
                 normalise(scored_at[k - 3])
-            reorder(k, "vector", nc.vector.tensor_copy)
+            if k != 0:
+                reorder(k, "vector", nc.vector.tensor_copy)
             reorder(k, "scalar", nc.scalar.copy)
             if k >= 0:
                 add_bias(k)

@@ -28,7 +28,7 @@ EARLY = 2
 EARLY_STEPS = S * EARLY
 STEPS = EARLY_STEPS + (ROW_TILES - EARLY) * S
 HALF = PACK // EARLY
-LOAD_LEAD = 10
+LOAD_LEAD = 14
 RUN = 8
 
 
@@ -38,9 +38,11 @@ def tile_tpru_pa_kernel(tc, h, x2f, vu, w_f, b_f, bh, bx, out):
     def first_step(i):
         return 0 if i < EARLY else EARLY_STEPS + (i - EARLY) * S
 
-    flips = {k: [] for k in range(-2, STEPS)}
-    flips[-2] = [("h", 0, 0), ("w", 0, 0), ("w", 0, 1)]
-    flips[-1] = [("h", 1, 0), ("w", 0, 2), ("w", 0, 3)]
+    head = [("h", 0, 0), ("w", 0, 0), ("w", 0, 1), ("h", 1, 0), ("w", 0, 2), ("w", 0, 3)]
+    FIRST = -len(head)
+    flips = {k: [] for k in range(FIRST, STEPS)}
+    for n, tile in enumerate(head):
+        flips[FIRST + n].append(tile)
     for s in range(1, S):
         for t in range(PACK):
             flips[EARLY * (s - 1) + t // HALF].append(("w", s, t))
@@ -67,6 +69,9 @@ def tile_tpru_pa_kernel(tc, h, x2f, vu, w_f, b_f, bh, bx, out):
 
         rows_of = {}
 
+        def parts_of(k):
+            return 2 if k < 0 else 1
+
         def load(k):
             for tile in flips.get(k, []):
                 kind, i, t = tile
@@ -79,10 +84,15 @@ def tile_tpru_pa_kernel(tc, h, x2f, vu, w_f, b_f, bh, bx, out):
                 else:
                     source = (h if kind == "h" else x2f)[i * P : (i + 1) * P, :]
                     rows = rows_pool.tile([P, D], BF16, tag=kind + "_rows", name="rows")
-                nc.sync.dma_start(out=rows[:], in_=source)
+                width = D // parts_of(k)
+                for column in range(0, D, width):
+                    nc.sync.dma_start(
+                        out=rows[:, column : column + width],
+                        in_=source[:, column : column + width],
+                    )
                 rows_of[tile] = rows
 
-        for k in range(-2, LOAD_LEAD - 3):
+        for k in range(FIRST, FIRST + LOAD_LEAD):
             load(k)
 
         ident = keep.tile([P, P], F32)
@@ -90,17 +100,13 @@ def tile_tpru_pa_kernel(tc, h, x2f, vu, w_f, b_f, bh, bx, out):
         bias_bf = keep.tile([P, S, PACK], BF16)
         nc.scalar.dma_start(out=bias_bf[:], in_=b_f.rearrange("(s p t) -> p s t", s=S, p=P))
         bias = keep.tile([P, S, PACK], F32)
-        nc.vector.tensor_copy(out=bias[:], in_=bias_bf[:])
         bh_bf = keep.tile([P, 1], BF16)
         nc.scalar.dma_start(out=bh_bf[:], in_=bh.partition_broadcast(P))
         bh_all = keep.tile([P, 1], F32)
-        nc.vector.tensor_copy(out=bh_all[:], in_=bh_bf[:])
         bx_bf = keep.tile([P, 1], BF16)
         nc.scalar.dma_start(out=bx_bf[:], in_=bx.partition_broadcast(P))
         bx_all = keep.tile([P, 1], F32)
-        nc.vector.tensor_copy(out=bx_all[:], in_=bx_bf[:])
         minus_bx = keep.tile([P, 1], F32)
-        nc.vector.tensor_scalar_mul(out=minus_bx[:], in0=bx_bf[:], scalar1=-1.0)
 
         vu_codes = keep.tile([P, S, N], U32, align_bytes=64)
         vu_scales = keep.tile([P, S, N], U8, align_bytes=64)
@@ -108,7 +114,7 @@ def tile_tpru_pa_kernel(tc, h, x2f, vu, w_f, b_f, bh, bx, out):
         w_scales = keep.tile([P, S, PACK, PASSES, P], U8, align_bytes=64)
 
         ordered_of = {}
-        flipped_at = {k: [] for k in range(-3, STEPS + 1)}
+        flipped_at = {k: [] for k in range(FIRST, STEPS)}
         packed = {}
         feat_of = {}
         f_grouped_of = {}
@@ -143,35 +149,41 @@ def tile_tpru_pa_kernel(tc, h, x2f, vu, w_f, b_f, bh, bx, out):
                 return "vector" if i < EARLY else "scalar"
             return None if kind == "vu" or i % 2 == 0 else "scalar"
 
-        def words_by_half(tile):
-            words = rows_of[tile][:].bitcast(F32)
-            if tile[0] in ("h", "w"):
-                return words.rearrange("r (b u i) -> r u b i", u=HALVES, i=RUN)
-            return words.rearrange("r (b u) -> r u b", u=HALVES)
+        def words_by_half(rows):
+            return rows.bitcast(F32).rearrange("r (b u) -> r u b", u=HALVES)
 
-        reorders = {k: [] for k in range(-4, STEPS)}
-        for k in range(-2, STEPS):
+        def runs_by_half(rows):
+            return rows.bitcast(F32).rearrange("r (b u i) -> r u b i", u=HALVES, i=RUN)
+
+        reorders = {k: [] for k in range(FIRST, STEPS)}
+        reorders["1"] = []
+        for k in range(FIRST, STEPS):
             for n, tile in enumerate(flips[k]):
                 if orderer(tile) == "vector":
-                    reorders[k - 1 if k not in (0, 1) else 0].append(tile)
+                    reorders[k - 1 if k > 1 else "1" if k == 1 else k].append((tile, parts_of(k)))
                 elif orderer(tile) == "scalar":
-                    reorders[k - 2].append(tile)
+                    reorders[k - 2 - (tile[0] == "x")].append((tile, 1))
 
         def reorder(k, who, copy):
-            for tile in reorders[k]:
+            for tile, parts in reorders[k]:
                 if orderer(tile) == who:
                     ordered = order_pool.tile(
                         [P, HALVES, PASSES * P], F32, tag="ordered_" + who, align_bytes=64
                     )
-                    laid = ordered[:]
-                    if tile[0] in ("h", "w"):
-                        laid = laid.rearrange("r u (b i) -> r u b i", i=RUN)
-                    copy(out=laid, in_=words_by_half(tile))
+                    width = PASSES * P // parts
+                    for n in range(parts):
+                        laid = ordered[:, :, n * width : (n + 1) * width]
+                        rows = rows_of[tile][:, n * D // parts : (n + 1) * D // parts]
+                        if tile[0] in ("h", "w"):
+                            laid = laid.rearrange("r u (b i) -> r u b i", i=RUN)
+                            copy(out=laid, in_=runs_by_half(rows))
+                        else:
+                            copy(out=laid, in_=words_by_half(rows))
                     ordered_of[tile] = ordered
 
         def flip(k):
             for tile in flips.get(k, []):
-                halves = ordered_of[tile][:] if tile in ordered_of else words_by_half(tile)
+                halves = ordered_of[tile][:] if tile in ordered_of else words_by_half(rows_of[tile][:])
                 grouped = flip_pool.tile([P, PASSES, P, HALVES], F32, align_bytes=64)
                 for first in range(0, PASSES, 2):
                     flipped = flip_psum.tile([P, 2, HALVES, P], F32)
@@ -325,23 +337,32 @@ def tile_tpru_pa_kernel(tc, h, x2f, vu, w_f, b_f, bh, bx, out):
             squared = squared_of[i][0]
             inverse = inverse_of[i]
             share = work.tile([P, N, S], F32)
-            nc.vector.tensor_tensor(
-                out=share[:],
-                in0=squared[:].rearrange("p s n -> p n s"),
-                in1=inverse[:].unsqueeze(1).to_broadcast([P, N, S]),
-                op=ALU.mult,
-            )
-            nc.sync.dma_start(
-                out=out[i * P : (i + 1) * P].rearrange("b n s -> b (n s)"),
-                in_=share[:].rearrange("p n s -> p (n s)"),
-            )
+            width = N // 2 if i == ROW_TILES - 1 else N
+            for n in range(0, N, width):
+                nc.vector.tensor_tensor(
+                    out=share[:, n : n + width, :],
+                    in0=squared[:, :, n : n + width].rearrange("p s n -> p n s"),
+                    in1=inverse[:].unsqueeze(1).to_broadcast([P, width, S]),
+                    op=ALU.mult,
+                )
+                nc.sync.dma_start(
+                    out=out[i * P : (i + 1) * P, n : n + width].rearrange("b n s -> b (n s)"),
+                    in_=share[:, n : n + width, :].rearrange("p n s -> p (n s)"),
+                )
 
         score_step = {i: first_step(i) + S + 2 for i in range(EARLY, ROW_TILES - 1)}
+        score_step[ROW_TILES - 2] = STEPS - 3
         for i in range(EARLY):
             score_step[i] = first_step(EARLY + i) + S + 3
         scored_at = {k: i for i, k in score_step.items()}
         LAST = ROW_TILES - 1
-        for k in range(-3, STEPS):
+        for k in range(FIRST, 0):
+            load(k + LOAD_LEAD)
+            reorder(k, "vector", nc.vector.tensor_copy)
+            quantise_flipped(k - 2)
+            flip(k)
+            reorder(k, "scalar", nc.scalar.copy)
+        for k in range(STEPS):
             load(k + LOAD_LEAD)
             if k - 3 in scored_at:
                 floor_total(scored_at[k - 3])
@@ -350,16 +371,23 @@ def tile_tpru_pa_kernel(tc, h, x2f, vu, w_f, b_f, bh, bx, out):
             quantise_features(k - 1)
             if k - 3 in scored_at:
                 invert(scored_at[k - 3])
+            if k == 0:
+                quantise_flipped(-2)
+                reorder(0, "vector", nc.vector.tensor_copy)
             quantise_flipped(k - 1)
             if k == 0:
-                reorder(k, "vector", nc.vector.tensor_copy)
-            if k >= 0:
-                features(k)
+                reorder("1", "vector", nc.vector.tensor_copy)
+                nc.vector.tensor_copy(out=bias[:], in_=bias_bf[:])
+                nc.vector.tensor_copy(out=bh_all[:], in_=bh_bf[:])
+                nc.vector.tensor_copy(out=bx_all[:], in_=bx_bf[:])
+                nc.vector.tensor_scalar_mul(out=minus_bx[:], in0=bx_bf[:], scalar1=-1.0)
+            features(k)
             if k in scored_at:
                 scores_of_x(scored_at[k])
                 scores_of_features(scored_at[k], range(S))
-            if k == STEPS - 1:
+            if k == STEPS - 2:
                 scores_of_x(LAST)
+            if k == STEPS - 1:
                 scores_of_features(LAST, range(S - 1))
             if k - 2 in scored_at:
                 square(scored_at[k - 2])
@@ -369,9 +397,7 @@ def tile_tpru_pa_kernel(tc, h, x2f, vu, w_f, b_f, bh, bx, out):
             if k != 0:
                 reorder(k, "vector", nc.vector.tensor_copy)
             reorder(k, "scalar", nc.scalar.copy)
-            if k >= 0:
-                add_bias(k)
-        square(LAST - 1)
+            add_bias(k)
         combine(LAST, 0, S - 2)
         quantise_features(STEPS - 1)
         scores_of_features(LAST, (S - 1,))

@@ -70,7 +70,7 @@ def tile_tpru_pa_kernel(tc, h, x2f, vu, w_f, b_f, bh, bx, out):
         rows_of = {}
 
         def parts_of(k):
-            return 2 if k < 0 else 1
+            return 1
 
         def load(k):
             for tile in flips.get(k, []):

@@ -350,17 +350,27 @@ def tile_tpru_pa_kernel(tc, h, x2f, vu, w_f, b_f, bh, bx, out):
                     in_=share[:, n : n + width, :].rearrange("p n s -> p (n s)"),
                 )
 
+        zeros = keep.tile([P, PACK * P], BF16)
+        nc.vector.memset(zeros[:], 0.0)
+
+        def warm_up(count):
+            feat = feat_psum.tile([P, PACK * P], F32)
+            for n in range(count):
+                nc.tensor.matmul(feat[:], zeros[:, :P], zeros[:], start=True, stop=True)
+
         score_step = {i: first_step(i) + S + 2 for i in range(EARLY, ROW_TILES - 1)}
         score_step[ROW_TILES - 2] = STEPS - 3
         for i in range(EARLY):
             score_step[i] = first_step(EARLY + i) + S + 3
         scored_at = {k: i for i, k in score_step.items()}
         LAST = ROW_TILES - 1
+        warm_up(8)
         for k in range(FIRST, 0):
             load(k + LOAD_LEAD)
             reorder(k, "vector", nc.vector.tensor_copy)
             quantise_flipped(k - 2)
             flip(k)
+            warm_up(1)
             reorder(k, "scalar", nc.scalar.copy)
         for k in range(STEPS):
             load(k + LOAD_LEAD)

@@ -50,8 +50,7 @@ def tile_tpru_pa_kernel(tc, h, x2f, vu, w_f, b_f, bh, bx, out):
     flips[EARLY_STEPS - 1] = [("x", EARLY, 0)]
     for i in range(EARLY + 1, ROW_TILES):
         flips[first_step(i) - 3] = [("h", i, 0), ("x", i, 0)]
-    for i in range(EARLY):
-        flips[first_step(EARLY + i) + 3] = [("x", i, 0)]
+    flips[first_step(EARLY) + 3] = [("x", i, 0) for i in range(EARLY)]
 
     with ExitStack() as ctx:
         keep = ctx.enter_context(tc.tile_pool(name="keep", bufs=1))
@@ -147,7 +146,7 @@ def tile_tpru_pa_kernel(tc, h, x2f, vu, w_f, b_f, bh, bx, out):
                 return "scalar" if i > 1 and t == PACK - 1 else "vector"
             if kind == "h":
                 return "vector" if i < EARLY else "scalar"
-            return None if kind == "vu" or i % 2 == 0 else "scalar"
+            return "vector" if kind == "vu" else None if i in (0, 2) else "scalar"
 
         def words_by_half(rows):
             return rows.bitcast(F32).rearrange("r (b u) -> r u b", u=HALVES)
@@ -408,10 +407,10 @@ def tile_tpru_pa_kernel(tc, h, x2f, vu, w_f, b_f, bh, bx, out):
                 reorder(k, "vector", nc.vector.tensor_copy)
             reorder(k, "scalar", nc.scalar.copy)
             add_bias(k)
-        combine(LAST, 0, S - 2)
+        combine(LAST, 0, 1)
         quantise_features(STEPS - 1)
         scores_of_features(LAST, (S - 1,))
-        combine(LAST, S - 2, S - 1)
+        combine(LAST, 1, S - 1)
         square(LAST, 0, S - 1)
         floor_total(LAST - 1)
         invert(LAST - 1)

@@ -122,7 +122,6 @@ def tile_tpru_pa_kernel(tc, h, x2f, vu, w_f, b_f, bh, bx, out):
         ax_of = {}
         both_of = {}
         squared_of = {}
-        floored_of = {}
         inverse_of = {}
 
         def packed_for(tile):
@@ -321,15 +320,9 @@ def tile_tpru_pa_kernel(tc, h, x2f, vu, w_f, b_f, bh, bx, out):
                     accum_out=total[:, s : s + 1],
                 )
 
-        def floor_total(i):
-            total = squared_of[i][1]
-            floored = work.tile([P, S], F32)
-            nc.vector.tensor_scalar_max(out=floored[:], in0=total[:], scalar1=EPS)
-            floored_of[i] = floored
-
         def invert(i):
             inverse = work.tile([P, S], F32)
-            nc.vector.reciprocal(out=inverse[:], in_=floored_of[i][:])
+            nc.vector.reciprocal(out=inverse[:], in_=squared_of[i][1][:])
             inverse_of[i] = inverse
 
         def normalise(i):
@@ -338,11 +331,13 @@ def tile_tpru_pa_kernel(tc, h, x2f, vu, w_f, b_f, bh, bx, out):
             share = work.tile([P, N, S], F32)
             width = N // 2 if i == ROW_TILES - 1 else N
             for n in range(0, N, width):
-                nc.vector.tensor_tensor(
+                nc.vector.scalar_tensor_tensor(
                     out=share[:, n : n + width, :],
-                    in0=squared[:, :, n : n + width].rearrange("p s n -> p n s"),
-                    in1=inverse[:].unsqueeze(1).to_broadcast([P, width, S]),
-                    op=ALU.mult,
+                    in0=inverse[:].unsqueeze(1).to_broadcast([P, width, S]),
+                    scalar=1.0 / EPS,
+                    in1=squared[:, :, n : n + width].rearrange("p s n -> p n s"),
+                    op0=ALU.min,
+                    op1=ALU.mult,
                 )
                 nc.sync.dma_start(
                     out=out[i * P : (i + 1) * P, n : n + width].rearrange("b n s -> b (n s)"),
@@ -373,8 +368,6 @@ def tile_tpru_pa_kernel(tc, h, x2f, vu, w_f, b_f, bh, bx, out):
             reorder(k, "scalar", nc.scalar.copy)
         for k in range(STEPS):
             load(k + LOAD_LEAD)
-            if k - 3 in scored_at:
-                floor_total(scored_at[k - 3])
             if k - 1 in scored_at:
                 combine(scored_at[k - 1])
             quantise_features(k - 1)
@@ -412,11 +405,9 @@ def tile_tpru_pa_kernel(tc, h, x2f, vu, w_f, b_f, bh, bx, out):
         scores_of_features(LAST, (S - 1,))
         combine(LAST, 1, S - 1)
         square(LAST, 0, S - 1)
-        floor_total(LAST - 1)
         invert(LAST - 1)
         combine(LAST, S - 1, S)
         square(LAST, S - 1, S)
         normalise(LAST - 1)
-        floor_total(LAST)
         invert(LAST)
         normalise(LAST)

from contextlib import ExitStack

import concourse.mybir as mybir
from concourse.masks import make_identity

F32 = mybir.dt.float32
BF16 = mybir.dt.bfloat16
U32 = mybir.dt.uint32
U8 = mybir.dt.uint8
FP8X4 = mybir.dt.float8_e4m3fn_x4
ACT = mybir.ActivationFunctionType
ALU = mybir.AluOpType

P = 128
PACK = 4
HALVES = 2
K_PASS = P * PACK

B, D, S, N = 1024, 2048, 4, 128
DS = D // S
PASSES = D // K_PASS
ROW_TILES = B // P
EPS = 1e-12

FLOPS = 2 * B * D * D + 2 * (2 * B * D * N)

EARLY = 2
EARLY_STEPS = S * EARLY
STEPS = EARLY_STEPS + (ROW_TILES - EARLY) * S
HALF = PACK // EARLY
LOAD_LEAD = 14
RUN = 8


def tile_tpru_pa_kernel(tc, h, x2f, vu, w_f, b_f, bh, bx, out):
    nc = tc.nc

    def first_step(i):
        return 0 if i < EARLY else EARLY_STEPS + (i - EARLY) * S

    head = [("h", 0, 0), ("w", 0, 0), ("w", 0, 1), ("h", 1, 0), ("w", 0, 2), ("w", 0, 3)]
    FIRST = -len(head)
    flips = {k: [] for k in range(FIRST, STEPS)}
    for n, tile in enumerate(head):
        flips[FIRST + n].append(tile)
    for s in range(1, S):
        for t in range(PACK):
            flips[EARLY * (s - 1) + t // HALF].append(("w", s, t))
    flips[EARLY_STEPS - 2] = [("h", EARLY, 0), ("vu", 0, 0)]
    flips[EARLY_STEPS - 1] = [("x", EARLY, 0)]
    for i in range(EARLY + 1, ROW_TILES):
        flips[first_step(i) - 3] = [("h", i, 0), ("x", i, 0)]
    flips[first_step(EARLY) + 3] = [("x", i, 0) for i in range(EARLY)]

    with ExitStack() as ctx:
        keep = ctx.enter_context(tc.tile_pool(name="keep", bufs=1))
        rows_pool = ctx.enter_context(tc.tile_pool(name="rows_pool", bufs=4))
        w_pool = ctx.enter_context(tc.tile_pool(name="w_pool", bufs=3 * PACK))
        order_pool = ctx.enter_context(tc.tile_pool(name="order_pool", bufs=3))
        flip_pool = ctx.enter_context(tc.tile_pool(name="flip_pool", bufs=6))
        code_pool = ctx.enter_context(tc.tile_pool(name="code_pool", bufs=4))
        feat_pool = ctx.enter_context(tc.tile_pool(name="feat_pool", bufs=4))
        fcode_pool = ctx.enter_context(tc.tile_pool(name="fcode_pool", bufs=(EARLY + 3) * S))
        work = ctx.enter_context(tc.tile_pool(name="work", bufs=3))
        flip_psum = ctx.enter_context(tc.psum_pool(name="flip_psum", bufs=4))
        feat_psum = ctx.enter_context(tc.psum_pool(name="feat_psum", bufs=4))
        ctx.enter_context(tc.manual_schedule())

        rows_of = {}

        def parts_of(k):
            return 1

        def load(k):
            for tile in flips.get(k, []):
                kind, i, t = tile
                if kind == "w":
                    source = w_f[i * DS : (i + 1) * DS, :].rearrange("(r t) k -> t r k", t=PACK)[t]
                    rows = w_pool.tile([P, D], BF16, tag="w_rows", name="w_rows")
                elif kind == "vu":
                    source = vu.rearrange("n s d -> n (s d)")
                    rows = keep.tile([P, D], BF16, name="vu_rows")
                else:
                    source = (h if kind == "h" else x2f)[i * P : (i + 1) * P, :]
                    rows = rows_pool.tile([P, D], BF16, tag=kind + "_rows", name="rows")
                width = D // parts_of(k)
                for column in range(0, D, width):
                    nc.sync.dma_start(
                        out=rows[:, column : column + width],
                        in_=source[:, column : column + width],
                    )
                rows_of[tile] = rows

        for k in range(FIRST, FIRST + LOAD_LEAD):
            load(k)

        ident = keep.tile([P, P], F32)
        make_identity(nc, ident[:])
        bias_bf = keep.tile([P, S, PACK], BF16)
        nc.scalar.dma_start(out=bias_bf[:], in_=b_f.rearrange("(s p t) -> p s t", s=S, p=P))
        bias = keep.tile([P, S, PACK], F32)
        bh_bf = keep.tile([P, 1], BF16)
        nc.scalar.dma_start(out=bh_bf[:], in_=bh.partition_broadcast(P))
        bh_all = keep.tile([P, 1], F32)
        bx_bf = keep.tile([P, 1], BF16)
        nc.scalar.dma_start(out=bx_bf[:], in_=bx.partition_broadcast(P))
        bx_all = keep.tile([P, 1], F32)
        minus_bx = keep.tile([P, 1], F32)

        vu_codes = keep.tile([P, S, N], U32, align_bytes=64)
        vu_scales = keep.tile([P, S, N], U8, align_bytes=64)
        w_codes = keep.tile([P, S, PACK, PASSES, P], U32, align_bytes=64)
        w_scales = keep.tile([P, S, PACK, PASSES, P], U8, align_bytes=64)

        ordered_of = {}
        flipped_at = {k: [] for k in range(FIRST, STEPS)}
        packed = {}
        feat_of = {}
        f_grouped_of = {}
        f_packed = {}
        relu_h_of = {}
        ax_of = {}
        both_of = {}
        squared_of = {}
        inverse_of = {}

        def packed_for(tile):
            kind, i, t = tile
            if kind == "w":
                return w_codes[:, i, t], w_scales[:, i, t]
            if kind == "vu":
                return vu_codes[:], vu_scales[:]
            codes = code_pool.tile(
                [P, PASSES, P], U32, tag=kind + "_codes", name="codes", align_bytes=64
            )
            scales = code_pool.tile(
                [P, PASSES, P], U8, tag=kind + "_scales", name="scales", align_bytes=64
            )
            packed[(kind, i)] = (codes, scales)
            return codes[:], scales[:]

        def orderer(tile):
            kind, i, t = tile
            if kind == "w":
                return "scalar" if i > 1 and t == PACK - 1 else "vector"
            if kind == "h":
                return "vector" if i < EARLY else "scalar"
            return "vector" if kind == "vu" else None if i in (0, 2) else "scalar"

        def words_by_half(rows):
            return rows.bitcast(F32).rearrange("r (b u) -> r u b", u=HALVES)

        def runs_by_half(rows):
            return rows.bitcast(F32).rearrange("r (b u i) -> r u b i", u=HALVES, i=RUN)

        reorders = {k: [] for k in range(FIRST, STEPS)}
        reorders["1"] = []
        for k in range(FIRST, STEPS):
            for n, tile in enumerate(flips[k]):
                if orderer(tile) == "vector":
                    reorders[k - 1 if k > 1 else "1" if k == 1 else k].append((tile, parts_of(k)))
                elif orderer(tile) == "scalar":
                    reorders[k - 2 - (tile[0] == "x")].append((tile, 1))

        def reorder(k, who, copy):
            for tile, parts in reorders[k]:
                if orderer(tile) == who:
                    ordered = order_pool.tile(
                        [P, HALVES, PASSES * P], F32, tag="ordered_" + who, align_bytes=64
                    )
                    width = PASSES * P // parts
                    for n in range(parts):
                        laid = ordered[:, :, n * width : (n + 1) * width]
                        rows = rows_of[tile][:, n * D // parts : (n + 1) * D // parts]
                        if tile[0] in ("h", "w"):
                            laid = laid.rearrange("r u (b i) -> r u b i", i=RUN)
                            copy(out=laid, in_=runs_by_half(rows))
                        else:
                            copy(out=laid, in_=words_by_half(rows))
                    ordered_of[tile] = ordered

        def flip(k):
            for tile in flips.get(k, []):
                halves = ordered_of[tile][:] if tile in ordered_of else words_by_half(rows_of[tile][:])
                grouped = flip_pool.tile([P, PASSES, P, HALVES], F32, align_bytes=64)
                for first in range(0, PASSES, 2):
                    flipped = flip_psum.tile([P, 2, HALVES, P], F32)
                    for g in range(2):
                        for u in range(HALVES):
                            nc.tensor.transpose(
                                flipped[:, g, u, :],
                                halves[:, u, (first + g) * P : (first + g + 1) * P],
                                ident[:],
                            )
                    nc.scalar.copy(
                        out=grouped[:, first : first + 2, :, :],
                        in_=flipped[:].rearrange("q g u r -> q g r u"),
                    )
                flipped_at[k].append((tile, grouped))

        def quantise_flipped(k):
            for tile, grouped in flipped_at.get(k, []):
                codes, scales = packed_for(tile)
                nc.vector.quantize_mx(
                    out=codes.rearrange("q g r -> q (g r)").bitcast(FP8X4),
                    scales=scales.rearrange("q g r -> q (g r)"),
                    in_=grouped[:].rearrange("q g r u -> q (g r u)").bitcast(BF16),
                )

        def step_work(k):
            if k < EARLY_STEPS:
                half = k % EARLY
                return range(EARLY), k // EARLY, range(half * HALF, (half + 1) * HALF)
            i, s = divmod(k - EARLY_STEPS, S)
            return (i + EARLY,), s, range(PACK)

        def finished(k):
            if not 0 <= k < STEPS:
                return []
            row_tiles, s, tiles = step_work(k)
            return [(i, s) for i in row_tiles] if PACK - 1 in tiles else []

        def features(k):
            row_tiles, s, tiles = step_work(k)
            for i in row_tiles:
                if 0 in tiles:
                    feat = feat_psum.tile([P, PACK, P], F32)
                    feat_of[(i, s)] = feat
            for t in tiles:
                for g in range(PASSES):
                    for i in row_tiles:
                        h_codes, h_scales = packed[("h", i)]
                        nc.tensor.matmul_mx(
                            out=feat_of[(i, s)][:, t, :],
                            lhsT=w_codes[:, s, t, g, :].bitcast(FP8X4),
                            lhsT_scale=w_scales[:, s, t, g, :],
                            rhs=h_codes[:, g, :].bitcast(FP8X4),
                            rhs_scale=h_scales[:, g, :],
                            start=(g == 0),
                            stop=(g == PASSES - 1),
                        )

        def add_bias(k):
            for i, s in finished(k):
                f_grouped = feat_pool.tile([P, P, PACK], BF16, align_bytes=64)
                nc.vector.tensor_tensor(
                    out=f_grouped[:],
                    in0=feat_of[(i, s)][:].rearrange("p t b -> p b t"),
                    in1=bias[:, s, :].unsqueeze(1).to_broadcast([P, P, PACK]),
                    op=ALU.add,
                )
                f_grouped_of[(i, s)] = f_grouped

        def quantise_features(k):
            for i, s in finished(k):
                f_codes = fcode_pool.tile([P, P], U32, align_bytes=64)
                f_scales = fcode_pool.tile([P, P], U8, align_bytes=64)
                nc.vector.quantize_mx(
                    out=f_codes[:].bitcast(FP8X4),
                    scales=f_scales[:],
                    in_=f_grouped_of[(i, s)][:].rearrange("p b t -> p (b t)"),
                )
                f_packed[(i, s)] = (f_codes, f_scales)

        def score(out_scores, s, codes, scales):
            nc.tensor.matmul_mx(
                out=out_scores,
                lhsT=codes.bitcast(FP8X4),
                lhsT_scale=scales,
                rhs=vu_codes[:, s, :].bitcast(FP8X4),
                rhs_scale=vu_scales[:, s, :],
                start=True,
                stop=True,
            )

        def scores_of_x(i):
            x_codes, x_scales = packed[("x", i)]
            ah = flip_psum.tile([P, S, N], F32, tag="flipped")
            for s in range(S):
                score(ah[:, s, :], s, x_codes[:, s, :], x_scales[:, s, :])
            relu_h = work.tile([P, S, N], F32)
            nc.scalar.activation(
                out=relu_h[:], in_=ah[:], func=ACT.Relu, bias=bh_all[:], scale=1.0
            )
            relu_h_of[i] = relu_h

        def scores_of_features(i, slices):
            if 0 in slices:
                ax = flip_psum.tile([P, S, N], F32, tag="flipped")
                ax_of[i] = ax
            for s in slices:
                f_codes, f_scales = f_packed[(i, s)]
                score(ax_of[i][:, s, :], s, f_codes[:], f_scales[:])

        def combine(i, first=0, last=S):
            if first == 0:
                both = work.tile([P, S, N], F32)
                both_of[i] = both
            nc.vector.scalar_tensor_tensor(
                out=both_of[i][:, first:last, :],
                in0=ax_of[i][:, first:last, :],
                scalar=minus_bx[:],
                in1=relu_h_of[i][:, first:last, :],
                op0=ALU.max,
                op1=ALU.add,
            )

        def square(i, first=0, last=S):
            if first == 0:
                squared = work.tile([P, S, N], F32)
                total = work.tile([P, S], F32)
                squared_of[i] = (squared, total)
            squared, total = squared_of[i]
            for s in range(first, last):
                nc.scalar.activation(
                    out=squared[:, s, :],
                    in_=both_of[i][:, s, :],
                    func=ACT.Square,
                    bias=bx_all[:],
                    accum_out=total[:, s : s + 1],
                )

        def invert(i):
            inverse = work.tile([P, S], F32)
            nc.vector.reciprocal(out=inverse[:], in_=squared_of[i][1][:])
            inverse_of[i] = inverse

        def normalise(i):
            squared = squared_of[i][0]
            inverse = inverse_of[i]
            share = work.tile([P, N, S], F32)
            width = N // 2 if i == ROW_TILES - 1 else N
            for n in range(0, N, width):
                nc.vector.scalar_tensor_tensor(
                    out=share[:, n : n + width, :],
                    in0=inverse[:].unsqueeze(1).to_broadcast([P, width, S]),
                    scalar=1.0 / EPS,
                    in1=squared[:, :, n : n + width].rearrange("p s n -> p n s"),
                    op0=ALU.min,
                    op1=ALU.mult,
                )
                nc.sync.dma_start(
                    out=out[i * P : (i + 1) * P, n : n + width].rearrange("b n s -> b (n s)"),
                    in_=share[:, n : n + width, :].rearrange("p n s -> p (n s)"),
                )

        zeros = keep.tile([P, PACK * P], BF16)
        nc.vector.memset(zeros[:], 0.0)

        def warm_up(count):
            feat = feat_psum.tile([P, PACK * P], F32)
            for n in range(count):
                nc.tensor.matmul(feat[:], zeros[:, :P], zeros[:], start=True, stop=True)

        score_step = {i: first_step(i) + S + 2 for i in range(EARLY, ROW_TILES - 1)}
        score_step[ROW_TILES - 2] = STEPS - 3
        for i in range(EARLY):
            score_step[i] = first_step(EARLY + i) + S + 3
        scored_at = {k: i for i, k in score_step.items()}
        LAST = ROW_TILES - 1
        warm_up(8)
        for k in range(FIRST, 0):
            load(k + LOAD_LEAD)
            reorder(k, "vector", nc.vector.tensor_copy)
            quantise_flipped(k - 2)
            flip(k)
            warm_up(1)
            reorder(k, "scalar", nc.scalar.copy)
        for k in range(STEPS):
            load(k + LOAD_LEAD)
            if k - 1 in scored_at:
                combine(scored_at[k - 1])
            quantise_features(k - 1)
            if k - 3 in scored_at:
                invert(scored_at[k - 3])
            if k == 0:
                quantise_flipped(-2)
                reorder(0, "vector", nc.vector.tensor_copy)
            quantise_flipped(k - 1)
            if k == 0:
                reorder("1", "vector", nc.vector.tensor_copy)
                nc.vector.tensor_copy(out=bias[:], in_=bias_bf[:])
                nc.vector.tensor_copy(out=bh_all[:], in_=bh_bf[:])
                nc.vector.tensor_copy(out=bx_all[:], in_=bx_bf[:])
                nc.vector.tensor_scalar_mul(out=minus_bx[:], in0=bx_bf[:], scalar1=-1.0)
            features(k)
            if k in scored_at:
                scores_of_x(scored_at[k])
                scores_of_features(scored_at[k], range(S))
            if k == STEPS - 2:
                scores_of_x(LAST)
            if k == STEPS - 1:
                scores_of_features(LAST, range(S - 1))
            if k - 2 in scored_at:
                square(scored_at[k - 2])
            flip(k)
            if k - 3 in scored_at:
                normalise(scored_at[k - 3])
            if k != 0:
                reorder(k, "vector", nc.vector.tensor_copy)
            reorder(k, "scalar", nc.scalar.copy)
            add_bias(k)
        combine(LAST, 0, 1)
        quantise_features(STEPS - 1)
        scores_of_features(LAST, (S - 1,))
        combine(LAST, 1, S - 1)
        square(LAST, 0, S - 1)
        invert(LAST - 1)
        combine(LAST, S - 1, S)
        square(LAST, S - 1, S)
        normalise(LAST - 1)
        invert(LAST)
        normalise(LAST)
